import numpy as np
import ml_dtypes


def mxq(x, axis, fmt="e4m3"):
    dtype, down = {"e4m3": (ml_dtypes.float8_e4m3fn, 7), "e5m2": (ml_dtypes.float8_e5m2, 14)}[fmt]
    v = np.moveaxis(np.asarray(x, np.float32).astype(ml_dtypes.bfloat16).astype(np.float64), axis, -1)
    blocks = v.reshape(v.shape[:-1] + (-1, 32))
    amax = np.abs(blocks).max(-1, keepdims=True)
    byte = np.maximum(np.where(amax > 0, np.frexp(amax)[1] - 1 + 127, 0) - down, 1)
    scale = np.exp2(byte - 127.0)
    codes = (blocks / scale).astype(np.float32).astype(dtype).astype(np.float64)
    return np.moveaxis((codes * scale).reshape(v.shape), -1, axis)


WIDE = False


def mx_kscale(k):
    if not WIDE:
        return np.ones(k)
    levels = np.array([10, -10, 5, -5, 0])
    if k % 512:
        return np.exp2(np.random.permutation(np.resize(levels, k // 32))).repeat(32)
    a = np.empty((k // 512, 16))
    for p in range(k // 512):
        a[p, :8] = np.random.permutation(np.resize(levels, 8))
        for g in range(8):
            far = levels[np.abs(levels - a[p, g]) >= 10]
            a[p, g + 8] = far[np.random.randint(len(far))]
    return np.exp2(a.ravel()).repeat(32)


BF16 = ml_dtypes.bfloat16


def bf(x):
    return np.asarray(x, np.float32).astype(BF16)


def f64(x):
    return np.asarray(x).astype(np.float64)


E2M1 = np.array([0.0, 0.5, 1.0, 1.5, 2.0, 3.0, 4.0, 6.0, -0.0, -0.5, -1.0, -1.5, -2.0, -3.0, -4.0, -6.0])


def pack_weight(w, fmt):
    k, n = w.shape
    w = f64(bf(w)).reshape(k // 32, 32, n)
    amax = np.abs(w).max(1)
    if fmt == "e4m3":
        byte = np.frexp(amax)[1] - 1 + 127 - 7
    else:
        mant, ex = np.frexp(amax / 6.0)
        byte = np.where(mant > 0.5, ex, ex - 1) + 127
    byte = np.clip(np.where(amax > 0, byte, 1), 1, 254)
    scaled = (w * np.exp2(127.0 - byte)[:, None, :]).reshape(k, n).astype(np.float32)
    by_word = np.ascontiguousarray(scaled.reshape(k // 512, 128, 4, n).transpose(0, 1, 3, 2))
    if fmt == "e4m3":
        words = by_word.astype(ml_dtypes.float8_e4m3fn).view(np.uint8)
    else:
        c = by_word.astype(ml_dtypes.float4_e2m1fn).view(np.uint8) & 0xF
        words = c[..., 0::2] | (c[..., 1::2] << 4)
    return np.ascontiguousarray(words), np.ascontiguousarray(byte.astype(np.uint8).reshape(k // 512, 16, n))


def unpack_weight(words, scales, fmt):
    g, p, n, _ = words.shape
    if fmt == "e4m3":
        vals = np.ascontiguousarray(words).view(ml_dtypes.float8_e4m3fn).astype(np.float64)
    else:
        nib = np.empty((g, p, n, 4), np.uint8)
        nib[..., 0::2] = words & 0xF
        nib[..., 1::2] = words >> 4
        vals = E2M1[nib]
    vals = vals * np.repeat(np.exp2(scales.astype(np.float64) - 127.0), 8, axis=1)[..., None]
    return vals.transpose(0, 1, 3, 2).reshape(g * 512, n)
def pack4(w):
    words, scales = pack_weight(w, "e2m1")
    return words.reshape(words.shape[0], 128, -1), scales


def unpack4(words, scales):
    return unpack_weight(words.reshape(words.shape[0], 128, -1, 2), scales, "e2m1")


B, S, D_MODEL, N_H, D_H, D_CQ, D_CKV, D_HR = 4, 1024, 1024, 4, 128, 512, 512, 128
ROPE_BASE = 10000.0


def rope_cos_sin(seq_len, dim):
    inv_freq = 1.0 / (ROPE_BASE ** (np.arange(0, dim, 2) / dim))
    ang = np.arange(seq_len)[:, None] * inv_freq[None, :]
    return np.cos(ang), np.sin(ang)


def rope(t, cos, sin):
    shp = t.shape
    d2 = shp[-1] // 2
    tr = t.reshape(shp[:-1] + (d2, 2))
    x0, x1 = tr[..., 0], tr[..., 1]
    bshape = (1, shp[1]) + (1,) * (x0.ndim - 3) + (d2,)
    cs, sn = cos.reshape(bshape), sin.reshape(bshape)
    return np.stack([x0 * cs - x1 * sn, x0 * sn + x1 * cs], axis=-1).reshape(shp)


def draw0():
    s, t = mx_kscale(D_MODEL), mx_kscale(D_CQ)
    h = bf(np.random.standard_normal((B, S, D_MODEL)) * s)
    w_cq_words, w_cq_scales = pack4(np.random.standard_normal((D_MODEL, D_CQ)) / np.sqrt(D_MODEL) / s[:, None] * t)
    w_q_words, w_q_scales = pack4(np.random.standard_normal((D_CQ, N_H * D_H)) / np.sqrt(D_CQ) / t[:, None])
    w_qr_words, w_qr_scales = pack4(np.random.standard_normal((D_CQ, N_H * D_HR)) / np.sqrt(D_CQ) / t[:, None])
    return {"h": h,
            "w_cq_words": w_cq_words, "w_cq_scales": w_cq_scales,
            "w_q_words": w_q_words, "w_q_scales": w_q_scales,
            "w_qr_words": w_qr_words, "w_qr_scales": w_qr_scales}


def core(h, w_cq_words, w_cq_scales, w_q_words, w_q_scales, w_qr_words, w_qr_scales):
    cos, sin = rope_cos_sin(S, D_HR)
    c_q = mxq(f64(h), 2, "e4m3") @ unpack4(w_cq_words, w_cq_scales)
    cq = mxq(c_q, 2, "e4m3")
    q_c = (cq @ unpack4(w_q_words, w_q_scales)).reshape(B, S, N_H, D_H).transpose(0, 2, 1, 3)
    q_r = rope((cq @ unpack4(w_qr_words, w_qr_scales)).reshape(B, S, N_H, D_HR), cos, sin).transpose(0, 2, 1, 3)
    return np.concatenate([q_c, q_r], axis=-1)


def e4m3fn_bytes(y):
    return np.clip(np.asarray(y, np.float64), -448.0, 448.0).astype(np.float32).astype(ml_dtypes.float8_e4m3fn).view(np.uint8)


def e4m3fn_values(b):
    return np.asarray(b, np.uint8).view(ml_dtypes.float8_e4m3fn).astype(np.float64)


def setup_inputs():
    d = draw0()
    x0 = np.asarray(d['h']).astype(np.float64)
    s = (np.max(np.abs(x0), axis=(0, 1), keepdims=True) / 448.0).astype(np.float32)
    out = {}
    for k, v in d.items():
        if k == 'h':
            out['h_bytes'] = e4m3fn_bytes(x0 / s.astype(np.float64))
            out['h_scale'] = s
        else:
            out[k] = v
    return out


def reference(h_bytes, h_scale, w_cq_words, w_cq_scales, w_q_words, w_q_scales, w_qr_words, w_qr_scales):
    return core(e4m3fn_values(h_bytes) * h_scale.astype(np.float64), w_cq_words, w_cq_scales, w_q_words, w_q_scales, w_qr_words, w_qr_scales)

@@ -1,0 +1,246 @@
+from contextlib import ExitStack
+
+import concourse.mybir as mybir
+from concourse.masks import make_identity
+
+B, S, D, NH, DH, CQ, HR = 4, 1024, 1024, 4, 128, 512, 128
+FLOPS = 2 * B * S * (D * CQ + CQ * NH * DH + CQ * NH * HR)
+
+F32 = mybir.dt.float32
+BF16 = mybir.dt.bfloat16
+U32 = mybir.dt.uint32
+I32 = mybir.dt.int32
+U8 = mybir.dt.uint8
+FP8 = mybir.dt.float8_e4m3fn
+FP8X4 = mybir.dt.float8_e4m3fn_x4
+FP4X4 = mybir.dt.float4_e2m1fn_x4
+ALU = mybir.AluOpType
+ACT = mybir.ActivationFunctionType
+
+P = 128
+J = 4
+GROUPS = B * S // (P * J)
+TILES = GROUPS * J
+TWO_PI = 6.283185307179586
+RATIO = 10000.0 ** (-1.0 / 64.0)
+
+
+def tile_mla_pa_t_w4_kernel(tc, h_bytes, h_scale, w_cq_words, w_cq_scales, w_q_words, w_q_scales, w_qr_words, w_qr_scales, out):
+    nc = tc.nc
+    with ExitStack() as ctx:
+        keep = ctx.enter_context(tc.tile_pool(name="keep", bufs=1))
+        xpool = ctx.enter_context(tc.tile_pool(name="xpool", bufs=GROUPS))
+        work = ctx.enter_context(tc.tile_pool(name="work", bufs=4))
+        outs = ctx.enter_context(tc.tile_pool(name="outs", bufs=3))
+        ps_tr = ctx.enter_context(tc.psum_pool(name="ps_tr", bufs=2))
+        ps_cq = ctx.enter_context(tc.psum_pool(name="ps_cq", bufs=2))
+        ps_u = ctx.enter_context(tc.psum_pool(name="ps_u", bufs=2))
+        ps_a = ctx.enter_context(tc.psum_pool(name="ps_a", bufs=2))
+
+        ident = keep.tile([P, P], F32, name="ident")
+        make_identity(nc, ident[:])
+
+        ctx.enter_context(tc.manual_schedule())
+
+        ws = keep.tile([P, 4, CQ], U8, name="ws", align_bytes=256)
+        nc.vector.memset(ws[:].rearrange("p a n -> p (a n)").bitcast(I32), 0)
+        sc = keep.tile([P, 8], F32, name="sc")
+        wraw = keep.tile([P, 2, 2 * CQ], U8, name="wraw", align_bytes=256)
+        wcw = keep.tile([P, 2, 2 * CQ], U8, name="wcw", align_bytes=256)
+        wcs = keep.tile([P, 2, CQ], U8, name="wcs", align_bytes=256)
+        wqw = keep.tile([P, 2, 2 * CQ], U8, name="wqw", align_bytes=256)
+
+        x_tiles = []
+        for k in range(GROUPS):
+            x_bytes = xpool.tile([P, J * D], U8, name="x_bytes", align_bytes=64)
+            x_tiles.append(x_bytes)
+        xs = [h_bytes[k // 2].rearrange("(f p j) d -> f p (j d)", p=P, j=J)[k % 2] for k in range(GROUPS)]
+        nc.sync.dma_start(out=x_tiles[0][:, 0:D], in_=xs[0][:, 0:D])
+        nc.sync.dma_start(out=wraw[:].bitcast(I32), in_=w_cq_words.rearrange("g p n -> p g n").bitcast(I32))
+        nc.sync.dma_start(out=sc[:].rearrange("p (g t) -> p g t", t=4), in_=h_scale.rearrange("a b (g p t) -> p (a b g) t", p=P, t=4))
+        nc.sync.dma_start(out=x_tiles[0][:, D : 2 * D], in_=xs[0][:, D : 2 * D])
+        for q in range(4):
+            nc.sync.dma_start(out=ws[32 * q : 32 * q + 4, 0:2, :].bitcast(I32), in_=w_cq_scales[:, 4 * q : 4 * q + 4, :].rearrange("g q n -> q g n").bitcast(I32))
+        nc.sync.dma_start(out=x_tiles[0][:, 2 * D : 4 * D], in_=xs[0][:, 2 * D : 4 * D])
+        for q in range(4):
+            nc.sync.dma_start(out=ws[32 * q : 32 * q + 4, 2, :].bitcast(I32), in_=w_q_scales[0, 4 * q : 4 * q + 4, :].bitcast(I32))
+            nc.sync.dma_start(out=ws[32 * q : 32 * q + 4, 3, :].bitcast(I32), in_=w_qr_scales[0, 4 * q : 4 * q + 4, :].bitcast(I32))
+        nc.sync.dma_start(out=wqw[:, 0, :].bitcast(I32), in_=w_q_words[0].bitcast(I32))
+        nc.sync.dma_start(out=wqw[:, 1, :].bitcast(I32), in_=w_qr_words[0].bitcast(I32))
+        for k in range(1, GROUPS):
+            nc.sync.dma_start(out=x_tiles[k][:], in_=xs[k])
+
+        zero = keep.tile([P, 1], F32, name="zero")
+        dummy = keep.tile([P, 1], F32, name="dummy")
+        nc.gpsimd.memset(zero[:], 0.0)
+        nc.scalar.activation(out=dummy[:], in_=zero[:], func=ACT.Sin)
+        pos = keep.tile([P, 8], F32, name="pos")
+        nc.gpsimd.iota(pos[:], pattern=[[512, 2], [1, 4]], base=0, channel_multiplier=4, allow_small_or_imprecise_dtypes=True)
+        turns = keep.tile([P, 2, 8, 64], F32, name="turns")
+        nc.gpsimd.tensor_scalar(turns[:, 1, :, 0:1], pos[:].rearrange("p (a o) -> p a o", o=1), 1.0 / TWO_PI, 0.0, ALU.mult, ALU.add)
+        w = 1
+        while w < 64:
+            nc.gpsimd.tensor_scalar(turns[:, 1, :, w : 2 * w], turns[:, 1, :, 0:w], RATIO**w, 0.0, ALU.mult, ALU.add)
+            w *= 2
+        nc.gpsimd.tensor_scalar(turns[:, 0, :, :], turns[:, 1, :, :], 1.0, 0.25, ALU.mult, ALU.add)
+        whole = keep.tile([P, 1024], I32, name="whole")
+        frac = keep.tile([P, 1024], F32, name="frac")
+        nfrac = keep.tile([P, 1024], F32, name="nfrac")
+        trig = keep.tile([P, 3, 8, 64], F32, name="trig")
+
+        for g in range(2):
+            nc.vector.tensor_copy(out=wcw[:, g, :].rearrange("p (t m b) -> p t m b", t=4, b=2), in_=wraw[:, g, :].rearrange("p (m t b) -> p t m b", t=4, b=2))
+        nc.vector.tensor_copy(out=wcs[:].rearrange("p g (t m) -> p g t m", t=4), in_=ws[:, 0:2, :].rearrange("p g (m t) -> p g t m", t=4))
+
+        hx, tr, hq, hc, hs, cq, cqb, cc, cs, aps, ups, m1, m2, osb = ({} for n in range(14))
+
+        def widen(i):
+            t_hx = work.tile([P, D], BF16, name="t_hx")
+            hx[i] = t_hx
+            nc.scalar.copy(out=t_hx[:], in_=x_tiles[i // J][:, (i % J) * D : (i % J + 1) * D].bitcast(FP8))
+
+        def turn(i):
+            t_tr = ps_tr.tile([P, 512], F32, name="t_tr")
+            tr[i] = t_tr
+            words = hx[i][:].bitcast(F32)
+            for u in range(2):
+                for g in range(2):
+                    c = (2 * u + g) * P
+                    nc.tensor.transpose(t_tr[:, c : c + P], words[:, 256 * g + u : 256 * (g + 1) : 2], ident[:])
+
+        def empty(i):
+            t_hq = work.tile([P, 2, P, 4], BF16, name="t_hq", align_bytes=64)
+            hq[i] = t_hq
+            src = tr[i][:].bitcast(BF16).rearrange("p (u g r e) -> p g r u e", u=2, g=2, e=2)
+            nc.vector.tensor_tensor(
+                out=t_hq[:].rearrange("p g r (u e) -> p g r u e", u=2),
+                in0=src,
+                in1=sc[:].rearrange("p (g o u e) -> p g o u e", g=2, o=1, u=2).to_broadcast([P, 2, P, 2, 2]),
+                op=ALU.mult,
+            )
+
+        def quant_h(i):
+            t_hc = work.tile([P, 2, P], U32, name="t_hc", align_bytes=64)
+            t_hs = work.tile([P, 2, P], U8, name="t_hs", align_bytes=64)
+            hc[i], hs[i] = t_hc, t_hs
+            nc.vector.quantize_mx(
+                out=t_hc[:].rearrange("p g r -> p (g r)").bitcast(FP8X4),
+                scales=t_hs[:].rearrange("p g r -> p (g r)"),
+                in_=hq[i][:].rearrange("p g r t -> p (g r t)"),
+            )
+
+        def mm1(i):
+            t_cq = ps_cq.tile([P, 4, P], F32, name="t_cq")
+            cq[i] = t_cq
+            for t in range(4):
+                for g in range(2):
+                    nc.tensor.matmul_mx(
+                        out=t_cq[:, t, :],
+                        lhsT=wcw[:, g, 256 * t : 256 * (t + 1)].bitcast(FP4X4),
+                        lhsT_scale=wcs[:, g, P * t : P * (t + 1)],
+                        rhs=hc[i][:, g, :].bitcast(FP8X4),
+                        rhs_scale=hs[i][:, g, :],
+                        start=(g == 0),
+                        stop=(g == 1),
+                    )
+
+        def copy_cq(i):
+            t_cqb = work.tile([P, P, 4], BF16, name="t_cqb", align_bytes=64)
+            cqb[i] = t_cqb
+            nc.scalar.copy(out=t_cqb[:], in_=cq[i][:].rearrange("p t n -> p n t"))
+
+        def quant_c(i):
+            t_cc = work.tile([P, P], U32, name="t_cc", align_bytes=64)
+            t_cs = work.tile([P, P], U8, name="t_cs", align_bytes=64)
+            cc[i], cs[i] = t_cc, t_cs
+            nc.vector.quantize_mx(out=t_cc[:].bitcast(FP8X4), scales=t_cs[:], in_=cqb[i][:].rearrange("p n t -> p (n t)"))
+
+        def mm2(i):
+            t_u = ps_u.tile([P, 512], F32, name="t_u")
+            t_a = ps_a.tile([P, 512], F32, name="t_a")
+            ups[i], aps[i] = t_u, t_a
+            for dst, which in ((t_u, 1), (t_a, 0)):
+                nc.tensor.matmul_mx(
+                    out=dst[:],
+                    lhsT=cc[i][:].bitcast(FP8X4),
+                    lhsT_scale=cs[i][:],
+                    rhs=wqw[:, which, :].bitcast(FP4X4),
+                    rhs_scale=ws[:, 2 + which, :],
+                    start=True,
+                    stop=True,
+                )
+
+        def copy_a(i):
+            if i % J == 0:
+                t_out = outs.tile([P, NH, J, 256], F32, name="t_out")
+                osb[i // J] = t_out
+            nc.scalar.copy(out=osb[i // J][:, :, i % J, 0:P], in_=aps[i][:].rearrange("p (n f) -> p n f", n=NH))
+
+        def rope_mul(i):
+            a = (i // J % 2) * J + i % J
+            t_m1 = work.tile([P, 512], F32, name="t_m1")
+            t_m2 = work.tile([P, 2, 256], F32, name="t_m2")
+            m1[i], m2[i] = t_m1, t_m2
+            u4 = ups[i][:].rearrange("p (n i e) -> p n i e", n=NH, e=2)
+            nc.vector.tensor_tensor(
+                out=t_m1[:].rearrange("p (n i e) -> p n i e", n=NH, e=2),
+                in0=u4,
+                in1=trig[:, 0, a, :].rearrange("p (o i q) -> p o i q", o=1, q=1).to_broadcast([P, NH, 64, 2]),
+                op=ALU.mult,
+            )
+            for e in range(2):
+                nc.vector.tensor_tensor(
+                    out=t_m2[:, e, :].rearrange("p (n i) -> p n i", n=NH),
+                    in0=u4[:, :, :, 1 - e],
+                    in1=trig[:, 2 - e, a, :].rearrange("p (o i) -> p o i", o=1).to_broadcast([P, NH, 64]),
+                    op=ALU.mult,
+                )
+
+        def rope_add(i):
+            nc.gpsimd.tensor_tensor(
+                out=osb[i // J][:, :, i % J, P : 2 * P].rearrange("p n (i e) -> p n i e", e=2),
+                in0=m1[i][:].rearrange("p (n i e) -> p n i e", n=NH, e=2),
+                in1=m2[i][:].rearrange("p e (n i) -> p n i e", n=NH),
+                op=ALU.add,
+            )
+
+        def store(i):
+            k = i // J
+            if i % 2 == 0 and k < GROUPS - 1:
+                return
+            dst = out[k // 2].rearrange("n (f p j) c -> f p n (j c)", p=P, j=J)[k % 2]
+            j0 = i % J if k == GROUPS - 1 else i % J - 1
+            j1 = i % J + 1
+            nc.sync.dma_start(out=dst[:, :, j0 * 256 : j1 * 256], in_=osb[k][:, :, j0:j1, :].rearrange("p n j c -> p n (j c)"))
+
+        def table_vector():
+            flat = turns[:].rearrange("p k a i -> p (k a i)")
+            nc.vector.tensor_copy(out=whole[:], in_=flat)
+            nc.vector.tensor_tensor(out=frac[:], in0=flat, in1=whole[:], op=ALU.subtract)
+            nc.vector.scalar_tensor_tensor(out=nfrac[:], in0=frac[:], scalar=0.5, in1=frac[:], op0=ALU.is_gt, op1=ALU.subtract)
+
+        def table_scalar():
+            nc.scalar.activation(out=trig[:, 0:2, :, :].rearrange("p k a i -> p (k a i)"), in_=nfrac[:], func=ACT.Sin, scale=-TWO_PI)
+            nc.scalar.activation(out=trig[:, 2, :, :].rearrange("p a i -> p (a i)"), in_=nfrac[:, 512:1024], func=ACT.Sin, scale=TWO_PI)
+
+        def at(fn, i):
+            if 0 <= i < TILES:
+                fn(i)
+
+        for s in range(TILES + 6):
+            at(widen, s)
+            at(quant_c, s - 4)
+            at(quant_h, s - 3)
+            at(mm2, s - 4)
+            at(rope_mul, s - 5)
+            at(empty, s - 2)
+            if s == 2:
+                table_vector()
+            if s == 3:
+                table_scalar()
+            at(copy_a, s - 4)
+            at(rope_add, s - 5)
+            at(mm1, s - 3)
+            at(copy_cq, s - 3)
+            at(turn, s - 1)
+            at(store, s - 5)

@@ -31,11 +31,12 @@ def tile_mla_pa_t_w4_kernel(tc, h_bytes, h_scale, w_cq_words, w_cq_scales, w_q_w
         keep = ctx.enter_context(tc.tile_pool(name="keep", bufs=1))
         xpool = ctx.enter_context(tc.tile_pool(name="xpool", bufs=GROUPS))
         work = ctx.enter_context(tc.tile_pool(name="work", bufs=4))
-        outs = ctx.enter_context(tc.tile_pool(name="outs", bufs=3))
+        outs = ctx.enter_context(tc.tile_pool(name="outs", bufs=5))
         ps_tr = ctx.enter_context(tc.psum_pool(name="ps_tr", bufs=2))
         ps_cq = ctx.enter_context(tc.psum_pool(name="ps_cq", bufs=2))
         ps_u = ctx.enter_context(tc.psum_pool(name="ps_u", bufs=2))
-        ps_a = ctx.enter_context(tc.psum_pool(name="ps_a", bufs=2))
+        ps_s = ctx.enter_context(tc.psum_pool(name="ps_s", bufs=1))
+        ps_a = ctx.enter_context(tc.psum_pool(name="ps_a", bufs=1))
 
         ident = keep.tile([P, P], F32, name="ident")
         make_identity(nc, ident[:])
@@ -49,6 +50,8 @@ def tile_mla_pa_t_w4_kernel(tc, h_bytes, h_scale, w_cq_words, w_cq_scales, w_q_w
         wcw = keep.tile([P, 2, 2 * CQ], U8, name="wcw", align_bytes=256)
         wcs = keep.tile([P, 2, CQ], U8, name="wcs", align_bytes=256)
         wqw = keep.tile([P, 2, 2 * CQ], U8, name="wqw", align_bytes=256)
+        wrw = keep.tile([P, 2 * CQ], U8, name="wrw", align_bytes=256)
+        wrs = keep.tile([P, CQ], U8, name="wrs", align_bytes=256)
 
         x_tiles = []
         for k in range(GROUPS):
@@ -76,23 +79,31 @@ def tile_mla_pa_t_w4_kernel(tc, h_bytes, h_scale, w_cq_words, w_cq_scales, w_q_w
         nc.scalar.activation(out=dummy[:], in_=zero[:], func=ACT.Sin)
         pos = keep.tile([P, 8], F32, name="pos")
         nc.gpsimd.iota(pos[:], pattern=[[512, 2], [1, 4]], base=0, channel_multiplier=4, allow_small_or_imprecise_dtypes=True)
-        turns = keep.tile([P, 2, 8, 64], F32, name="turns")
-        nc.gpsimd.tensor_scalar(turns[:, 1, :, 0:1], pos[:].rearrange("p (a o) -> p a o", o=1), 1.0 / TWO_PI, 0.0, ALU.mult, ALU.add)
+        turns = keep.tile([P, 8, 64], F32, name="turns")
+        nc.gpsimd.tensor_scalar(turns[:, :, 0:1], pos[:].rearrange("p (a o) -> p a o", o=1), 1.0 / TWO_PI, 0.0, ALU.mult, ALU.add)
         w = 1
         while w < 64:
-            nc.gpsimd.tensor_scalar(turns[:, 1, :, w : 2 * w], turns[:, 1, :, 0:w], RATIO**w, 0.0, ALU.mult, ALU.add)
+            nc.gpsimd.tensor_scalar(turns[:, :, w : 2 * w], turns[:, :, 0:w], RATIO**w, 0.0, ALU.mult, ALU.add)
             w *= 2
-        nc.gpsimd.tensor_scalar(turns[:, 0, :, :], turns[:, 1, :, :], 1.0, 0.25, ALU.mult, ALU.add)
-        whole = keep.tile([P, 1024], I32, name="whole")
-        frac = keep.tile([P, 1024], F32, name="frac")
-        nfrac = keep.tile([P, 1024], F32, name="nfrac")
+        whole = keep.tile([P, 512], I32, name="whole")
+        nc.gpsimd.tensor_scalar(whole[:], turns[:].rearrange("p a i -> p (a i)"), 1.0, 0.0, ALU.mult, ALU.add)
+        frac = keep.tile([P, 512], F32, name="frac")
+        nfrac = keep.tile([P, 512], F32, name="nfrac")
+        afrac = keep.tile([P, 512], F32, name="afrac")
         trig = keep.tile([P, 3, 8, 64], F32, name="trig")
+        pairs = keep.tile([P, 2, 8, 64], F32, name="pairs")
 
         for g in range(2):
             nc.vector.tensor_copy(out=wcw[:, g, :].rearrange("p (t m b) -> p t m b", t=4, b=2), in_=wraw[:, g, :].rearrange("p (m t b) -> p t m b", t=4, b=2))
         nc.vector.tensor_copy(out=wcs[:].rearrange("p g (t m) -> p g t m", t=4), in_=ws[:, 0:2, :].rearrange("p g (m t) -> p g t m", t=4))
 
-        hx, tr, hq, hc, hs, cq, cqb, cc, cs, aps, ups, m1, m2, osb = ({} for n in range(14))
+        def order_rope_weights():
+            nc.gpsimd.tensor_copy(out=wrw[:, 0:CQ].rearrange("p (q b) -> p q b", b=2), in_=wqw[:, 1, :].rearrange("p (q e b) -> p e q b", e=2, b=2)[:, 1])
+            nc.gpsimd.tensor_copy(out=wrw[:, CQ : 2 * CQ].rearrange("p (q b) -> p q b", b=2), in_=wqw[:, 1, :].rearrange("p (q e b) -> p e q b", e=2, b=2)[:, 0])
+            for e in range(2):
+                nc.gpsimd.tensor_copy(out=wrs[:, 256 * (1 - e) : 256 * (2 - e)], in_=ws[:, 3, :].rearrange("p (q e) -> p e q", e=2)[:, e])
+
+        hx, tr, hq, hc, hs, cq, cqb, cc, cs, aps, ups, sps, m1, m2, osb, opair = ({} for n in range(16))
 
         def widen(i):
             t_hx = work.tile([P, D], BF16, name="t_hx")
@@ -157,90 +168,106 @@ def tile_mla_pa_t_w4_kernel(tc, h_bytes, h_scale, w_cq_words, w_cq_scales, w_q_w
 
         def mm2(i):
             t_u = ps_u.tile([P, 512], F32, name="t_u")
+            t_s = ps_s.tile([P, 256], F32, name="t_s")
             t_a = ps_a.tile([P, 512], F32, name="t_a")
-            ups[i], aps[i] = t_u, t_a
-            for dst, which in ((t_u, 1), (t_a, 0)):
+            ups[i], sps[i], aps[i] = t_u, t_s, t_a
+
+            def product(dst, words, scales, start, stop):
                 nc.tensor.matmul_mx(
-                    out=dst[:],
+                    out=dst,
                     lhsT=cc[i][:].bitcast(FP8X4),
                     lhsT_scale=cs[i][:],
-                    rhs=wqw[:, which, :].bitcast(FP4X4),
-                    rhs_scale=ws[:, 2 + which, :],
-                    start=True,
-                    stop=True,
+                    rhs=words.bitcast(FP4X4),
+                    rhs_scale=scales,
+                    start=start,
+                    stop=stop,
                 )
 
+            product(t_u[:], wrw[:], wrs[:], True, True)
+            for c in range(2):
+                for e in range(2):
+                    n0 = 256 * e + P * c
+                    product(t_s[:, P * c : P * (c + 1)], wrw[:, 2 * n0 : 2 * n0 + 256], wrs[:, n0 : n0 + P], e == 0, e == 1)
+            product(t_a[:], wqw[:, 0, :], ws[:, 2, :], True, True)
+
         def copy_a(i):
-            if i % J == 0:
-                t_out = outs.tile([P, NH, J, 256], F32, name="t_out")
-                osb[i // J] = t_out
-            nc.scalar.copy(out=osb[i // J][:, :, i % J, 0:P], in_=aps[i][:].rearrange("p (n f) -> p n f", n=NH))
+            if i >= TILES - 2:
+                t_last = outs.tile([P, NH, 1, 256], F32, name="t_last")
+                osb[i] = t_last[:, :, 0, :]
+            elif i % 2 == 0:
+                t_out = outs.tile([P, NH, 2, 256], F32, name="t_out")
+                osb[i], osb[i + 1] = t_out[:, :, 0, :], t_out[:, :, 1, :]
+                opair[i + 1] = t_out
+            nc.scalar.copy(out=osb[i][:, :, 0:P], in_=aps[i][:].rearrange("p (n f) -> p n f", n=NH))
 
         def rope_mul(i):
             a = (i // J % 2) * J + i % J
-            t_m1 = work.tile([P, 512], F32, name="t_m1")
-            t_m2 = work.tile([P, 2, 256], F32, name="t_m2")
+            t_m1 = work.tile([P, 2, 256], F32, name="t_m1")
+            t_m2 = work.tile([P, 256], F32, name="t_m2")
             m1[i], m2[i] = t_m1, t_m2
-            u4 = ups[i][:].rearrange("p (n i e) -> p n i e", n=NH, e=2)
             nc.vector.tensor_tensor(
-                out=t_m1[:].rearrange("p (n i e) -> p n i e", n=NH, e=2),
-                in0=u4,
-                in1=trig[:, 0, a, :].rearrange("p (o i q) -> p o i q", o=1, q=1).to_broadcast([P, NH, 64, 2]),
+                out=m1[i][:].rearrange("p e (n i) -> p e n i", n=NH),
+                in0=ups[i][:].rearrange("p (e n i) -> p e n i", e=2, n=NH),
+                in1=pairs[:, :, a, :].rearrange("p e (o i) -> p e o i", o=1).to_broadcast([P, 2, NH, 64]),
                 op=ALU.mult,
             )
-            for e in range(2):
-                nc.vector.tensor_tensor(
-                    out=t_m2[:, e, :].rearrange("p (n i) -> p n i", n=NH),
-                    in0=u4[:, :, :, 1 - e],
-                    in1=trig[:, 2 - e, a, :].rearrange("p (o i) -> p o i", o=1).to_broadcast([P, NH, 64]),
-                    op=ALU.mult,
-                )
+            nc.vector.tensor_tensor(
+                out=m2[i][:].rearrange("p (n i) -> p n i", n=NH),
+                in0=sps[i][:].rearrange("p (n i) -> p n i", n=NH),
+                in1=trig[:, 0, a, :].rearrange("p (o i) -> p o i", o=1).to_broadcast([P, NH, 64]),
+                op=ALU.mult,
+            )
 
-        def rope_add(i):
-            nc.gpsimd.tensor_tensor(
-                out=osb[i // J][:, :, i % J, P : 2 * P].rearrange("p n (i e) -> p n i e", e=2),
-                in0=m1[i][:].rearrange("p (n i e) -> p n i e", n=NH, e=2),
-                in1=m2[i][:].rearrange("p e (n i) -> p n i e", n=NH),
+        def rope_add(i, eng):
+            eng.tensor_tensor(
+                out=osb[i][:, :, P : 2 * P].rearrange("p n (i e) -> p n i e", e=2),
+                in0=m1[i][:].rearrange("p e (n i) -> p n i e", n=NH),
+                in1=m2[i][:].rearrange("p (n i o) -> p n i o", n=NH, o=1).to_broadcast([P, NH, 64, 2]),
                 op=ALU.add,
             )
 
         def store(i):
-            k = i // J
-            if i % 2 == 0 and k < GROUPS - 1:
-                return
+            k, j = i // J, i % J
             dst = out[k // 2].rearrange("n (f p j) c -> f p n (j c)", p=P, j=J)[k % 2]
-            j0 = i % J if k == GROUPS - 1 else i % J - 1
-            j1 = i % J + 1
-            nc.sync.dma_start(out=dst[:, :, j0 * 256 : j1 * 256], in_=osb[k][:, :, j0:j1, :].rearrange("p n j c -> p n (j c)"))
+            if i >= TILES - 2:
+                nc.sync.dma_start(out=dst[:, :, j * 256 : (j + 1) * 256], in_=osb[i])
+            elif i % 2 == 1:
+                nc.sync.dma_start(out=dst[:, :, (j - 1) * 256 : (j + 1) * 256], in_=opair[i][:].rearrange("p n j c -> p n (j c)"))
 
         def table_vector():
-            flat = turns[:].rearrange("p k a i -> p (k a i)")
-            nc.vector.tensor_copy(out=whole[:], in_=flat)
+            flat = turns[:].rearrange("p a i -> p (a i)")
             nc.vector.tensor_tensor(out=frac[:], in0=flat, in1=whole[:], op=ALU.subtract)
             nc.vector.scalar_tensor_tensor(out=nfrac[:], in0=frac[:], scalar=0.5, in1=frac[:], op0=ALU.is_gt, op1=ALU.subtract)
 
         def table_scalar():
-            nc.scalar.activation(out=trig[:, 0:2, :, :].rearrange("p k a i -> p (k a i)"), in_=nfrac[:], func=ACT.Sin, scale=-TWO_PI)
-            nc.scalar.activation(out=trig[:, 2, :, :].rearrange("p a i -> p (a i)"), in_=nfrac[:, 512:1024], func=ACT.Sin, scale=TWO_PI)
+            flat = trig[:].rearrange("p k a i -> p k (a i)")
+            nc.scalar.activation(out=flat[:, 1, :], in_=nfrac[:], func=ACT.Sin, scale=TWO_PI)
+            nc.scalar.activation(out=flat[:, 2, :], in_=nfrac[:], func=ACT.Sin, scale=-TWO_PI)
+            nc.scalar.activation(out=afrac[:], in_=nfrac[:], func=ACT.Abs)
+            nc.scalar.activation(out=flat[:, 0, :], in_=afrac[:], func=ACT.Sin, scale=-TWO_PI, bias=TWO_PI / 4)
+            nc.gpsimd.tensor_tensor(out=pairs[:].rearrange("p k a i -> p k (a i)"), in0=flat[:, 1:3, :], in1=flat[:, 0:1, :].to_broadcast([P, 2, 512]), op=ALU.subtract)
 
         def at(fn, i):
             if 0 <= i < TILES:
                 fn(i)
 
-        for s in range(TILES + 6):
-            at(widen, s)
-            at(quant_c, s - 4)
-            at(quant_h, s - 3)
-            at(mm2, s - 4)
-            at(rope_mul, s - 5)
+        for s in range(TILES + 7):
+            at(copy_a, s - 6)
+            at(rope_mul, s - 6)
+            at(quant_c, s - 5)
             at(empty, s - 2)
-            if s == 2:
-                table_vector()
             if s == 3:
+                order_rope_weights()
+                table_vector()
+            if s == 4:
                 table_scalar()
-            at(copy_a, s - 4)
-            at(rope_add, s - 5)
-            at(mm1, s - 3)
-            at(copy_cq, s - 3)
+            if 0 <= s - 6 < TILES:
+                i = s - 6
+                rope_add(i, nc.vector if i >= TILES - 2 else nc.gpsimd)
+            at(quant_h, s - 3)
+            at(mm2, s - 5)
             at(turn, s - 1)
-            at(store, s - 5)
+            at(copy_cq, s - 4)
+            at(widen, s)
+            at(mm1, s - 3)
+            at(store, s - 6)

@@ -95,7 +95,6 @@ def tile_mla_pa_t_w4_kernel(tc, h_bytes, h_scale, w_cq_words, w_cq_scales, w_q_w
 
         for g in range(2):
             nc.vector.tensor_copy(out=wcw[:, g, :].rearrange("p (t m b) -> p t m b", t=4, b=2), in_=wraw[:, g, :].rearrange("p (m t b) -> p t m b", t=4, b=2))
-        nc.vector.tensor_copy(out=wcs[:].rearrange("p g (t m) -> p g t m", t=4), in_=ws[:, 0:2, :].rearrange("p g (m t) -> p g t m", t=4))
 
         def order_rope_weights():
             nc.gpsimd.tensor_copy(out=wrw[:, 0:CQ].rearrange("p (q b) -> p q b", b=2), in_=wqw[:, 1, :].rearrange("p (q e b) -> p e q b", e=2, b=2)[:, 1])
@@ -108,14 +107,18 @@ def tile_mla_pa_t_w4_kernel(tc, h_bytes, h_scale, w_cq_words, w_cq_scales, w_q_w
         def widen(i):
             t_hx = work.tile([P, D], BF16, name="t_hx")
             hx[i] = t_hx
-            nc.scalar.copy(out=t_hx[:], in_=x_tiles[i // J][:, (i % J) * D : (i % J + 1) * D].bitcast(FP8))
+            steps = 2 if i == 0 else 1
+            for c in range(steps):
+                w = D // steps
+                c0 = (i % J) * D + c * w
+                nc.scalar.copy(out=t_hx[:, c * w : (c + 1) * w], in_=x_tiles[i // J][:, c0 : c0 + w].bitcast(FP8))
 
         def turn(i):
             t_tr = ps_tr.tile([P, 512], F32, name="t_tr")
             tr[i] = t_tr
             words = hx[i][:].bitcast(F32)
-            for u in range(2):
-                for g in range(2):
+            for g in range(2):
+                for u in range(2):
                     c = (2 * u + g) * P
                     nc.tensor.transpose(t_tr[:, c : c + P], words[:, 256 * g + u : 256 * (g + 1) : 2], ident[:])
 
@@ -203,14 +206,18 @@ def tile_mla_pa_t_w4_kernel(tc, h_bytes, h_scale, w_cq_words, w_cq_scales, w_q_w
         def rope_mul(i):
             a = (i // J % 2) * J + i % J
             t_m1 = work.tile([P, 2, 256], F32, name="t_m1")
-            t_m2 = work.tile([P, 256], F32, name="t_m2")
-            m1[i], m2[i] = t_m1, t_m2
+            m1[i] = t_m1
             nc.vector.tensor_tensor(
                 out=m1[i][:].rearrange("p e (n i) -> p e n i", n=NH),
                 in0=ups[i][:].rearrange("p (e n i) -> p e n i", e=2, n=NH),
                 in1=pairs[:, :, a, :].rearrange("p e (o i) -> p e o i", o=1).to_broadcast([P, 2, NH, 64]),
                 op=ALU.mult,
             )
+
+        def rope_sum(i):
+            a = (i // J % 2) * J + i % J
+            t_m2 = work.tile([P, 256], F32, name="t_m2")
+            m2[i] = t_m2
             nc.vector.tensor_tensor(
                 out=m2[i][:].rearrange("p (n i) -> p n i", n=NH),
                 in0=sps[i][:].rearrange("p (n i) -> p n i", n=NH),
@@ -251,23 +258,26 @@ def tile_mla_pa_t_w4_kernel(tc, h_bytes, h_scale, w_cq_words, w_cq_scales, w_q_w
             if 0 <= i < TILES:
                 fn(i)
 
-        for s in range(TILES + 7):
-            at(copy_a, s - 6)
-            at(rope_mul, s - 6)
-            at(quant_c, s - 5)
+        for s in range(TILES + 6):
             at(empty, s - 2)
+            if s == 2:
+                nc.vector.tensor_copy(out=wcs[:].rearrange("p g (t m) -> p g t m", t=4), in_=ws[:, 0:2, :].rearrange("p g (m t) -> p g t m", t=4))
             if s == 3:
                 order_rope_weights()
                 table_vector()
             if s == 4:
                 table_scalar()
-            if 0 <= s - 6 < TILES:
-                i = s - 6
-                rope_add(i, nc.vector if i >= TILES - 2 else nc.gpsimd)
-            at(quant_h, s - 3)
-            at(mm2, s - 5)
-            at(turn, s - 1)
             at(copy_cq, s - 4)
+            at(copy_a, s - 5)
+            at(rope_mul, s - 5)
+            at(quant_h, s - 3)
+            at(quant_c, s - 4)
+            at(rope_sum, s - 5)
+            if 0 <= s - 5 < TILES:
+                i = s - 5
+                rope_add(i, nc.vector if i >= TILES - 2 else nc.gpsimd)
             at(widen, s)
+            at(turn, s - 1)
             at(mm1, s - 3)
-            at(store, s - 6)
+            at(mm2, s - 4)
+            at(store, s - 5)

@@ -30,12 +30,12 @@ def tile_mla_pa_t_w4_kernel(tc, h_bytes, h_scale, w_cq_words, w_cq_scales, w_q_w
     with ExitStack() as ctx:
         keep = ctx.enter_context(tc.tile_pool(name="keep", bufs=1))
         xpool = ctx.enter_context(tc.tile_pool(name="xpool", bufs=GROUPS))
-        work = ctx.enter_context(tc.tile_pool(name="work", bufs=4))
+        work = ctx.enter_context(tc.tile_pool(name="work", bufs=5))
         outs = ctx.enter_context(tc.tile_pool(name="outs", bufs=5))
-        ps_tr = ctx.enter_context(tc.psum_pool(name="ps_tr", bufs=2))
-        ps_cq = ctx.enter_context(tc.psum_pool(name="ps_cq", bufs=2))
-        ps_u = ctx.enter_context(tc.psum_pool(name="ps_u", bufs=2))
-        ps_s = ctx.enter_context(tc.psum_pool(name="ps_s", bufs=1))
+        ps_tr = ctx.enter_context(tc.psum_pool(name="ps_tr", bufs=3))
+        ps_cq = ctx.enter_context(tc.psum_pool(name="ps_cq", bufs=1))
+        ps_u = ctx.enter_context(tc.psum_pool(name="ps_u", bufs=1))
+        ps_s = ctx.enter_context(tc.psum_pool(name="ps_s", bufs=2))
         ps_a = ctx.enter_context(tc.psum_pool(name="ps_a", bufs=1))
 
         ident = keep.tile([P, P], F32, name="ident")
@@ -58,8 +58,9 @@ def tile_mla_pa_t_w4_kernel(tc, h_bytes, h_scale, w_cq_words, w_cq_scales, w_q_w
             x_bytes = xpool.tile([P, J * D], U8, name="x_bytes", align_bytes=64)
             x_tiles.append(x_bytes)
         xs = [h_bytes[k // 2].rearrange("(f p j) d -> f p (j d)", p=P, j=J)[k % 2] for k in range(GROUPS)]
+        nc.sync.dma_start(out=wraw[:, 0, :].bitcast(I32), in_=w_cq_words[0].bitcast(I32))
         nc.sync.dma_start(out=x_tiles[0][:, 0:D], in_=xs[0][:, 0:D])
-        nc.sync.dma_start(out=wraw[:].bitcast(I32), in_=w_cq_words.rearrange("g p n -> p g n").bitcast(I32))
+        nc.sync.dma_start(out=wraw[:, 1, :].bitcast(I32), in_=w_cq_words[1].bitcast(I32))
         nc.sync.dma_start(out=sc[:].rearrange("p (g t) -> p g t", t=4), in_=h_scale.rearrange("a b (g p t) -> p (a b g) t", p=P, t=4))
         nc.sync.dma_start(out=x_tiles[0][:, D : 2 * D], in_=xs[0][:, D : 2 * D])
         for q in range(4):
@@ -91,29 +92,50 @@ def tile_mla_pa_t_w4_kernel(tc, h_bytes, h_scale, w_cq_words, w_cq_scales, w_q_w
         nfrac = keep.tile([P, 512], F32, name="nfrac")
         afrac = keep.tile([P, 512], F32, name="afrac")
         trig = keep.tile([P, 3, 8, 64], F32, name="trig")
-        pairs = keep.tile([P, 2, 8, 64], F32, name="pairs")
+        pairs = keep.tile([P, 8, 64, 2], F32, name="pairs")
 
         for g in range(2):
             nc.vector.tensor_copy(out=wcw[:, g, :].rearrange("p (t m b) -> p t m b", t=4, b=2), in_=wraw[:, g, :].rearrange("p (m t b) -> p t m b", t=4, b=2))
 
-        def order_rope_weights():
-            nc.gpsimd.tensor_copy(out=wrw[:, 0:CQ].rearrange("p (q b) -> p q b", b=2), in_=wqw[:, 1, :].rearrange("p (q e b) -> p e q b", e=2, b=2)[:, 1])
-            nc.gpsimd.tensor_copy(out=wrw[:, CQ : 2 * CQ].rearrange("p (q b) -> p q b", b=2), in_=wqw[:, 1, :].rearrange("p (q e b) -> p e q b", e=2, b=2)[:, 0])
-            for e in range(2):
-                nc.gpsimd.tensor_copy(out=wrs[:, 256 * (1 - e) : 256 * (2 - e)], in_=ws[:, 3, :].rearrange("p (q e) -> p e q", e=2)[:, e])
+        def order_cq_scales():
+            nc.vector.tensor_copy(out=wcs[:].rearrange("p g (t m) -> p g t m", t=4), in_=ws[:, 0:2, :].rearrange("p g (m t) -> p g t m", t=4))
 
-        hx, tr, hq, hc, hs, cq, cqb, cc, cs, aps, ups, sps, m1, m2, osb, opair = ({} for n in range(16))
+        def order_rope_weights():
+            for e in range(2):
+                nc.vector.tensor_copy(out=wrw[:, CQ * (1 - e) : CQ * (2 - e)].rearrange("p (q b) -> p q b", b=2), in_=wqw[:, 1, :].rearrange("p (q e b) -> p e q b", e=2, b=2)[:, e])
+            for e in range(2):
+                nc.vector.tensor_copy(out=wrs[:, 256 * (1 - e) : 256 * (2 - e)], in_=ws[:, 3, :].rearrange("p (q e) -> p e q", e=2)[:, e])
+
+        def table_vector():
+            flat = turns[:].rearrange("p a i -> p (a i)")
+            nc.vector.tensor_tensor(out=frac[:], in0=flat, in1=whole[:], op=ALU.subtract)
+            nc.vector.scalar_tensor_tensor(out=nfrac[:], in0=frac[:], scalar=0.5, in1=frac[:], op0=ALU.is_gt, op1=ALU.subtract)
+
+        def table_scalar():
+            flat = trig[:].rearrange("p k a i -> p k (a i)")
+            nc.scalar.activation(out=flat[:, 1, :], in_=nfrac[:], func=ACT.Sin, scale=TWO_PI)
+            nc.scalar.activation(out=flat[:, 2, :], in_=nfrac[:], func=ACT.Sin, scale=-TWO_PI)
+            nc.scalar.activation(out=afrac[:], in_=nfrac[:], func=ACT.Abs)
+            nc.scalar.activation(out=flat[:, 0, :], in_=afrac[:], func=ACT.Sin, scale=-TWO_PI, bias=TWO_PI / 4)
+            nc.vector.tensor_tensor(
+                out=pairs[:].rearrange("p a i k -> p (a i) k"),
+                in0=flat[:, 1:3, :].rearrange("p k q -> p q k"),
+                in1=flat[:, 0, :].rearrange("p (q o) -> p q o", o=1).to_broadcast([P, 512, 2]),
+                op=ALU.subtract,
+            )
+
+        hx, tr, hq, hc, hs, cq, cqb, cc, cs, aps, ups, sps, mt, kt, osb, opair = ({} for n in range(16))
 
         def widen(i):
             t_hx = work.tile([P, D], BF16, name="t_hx")
             hx[i] = t_hx
             steps = 2 if i == 0 else 1
+            w = D // steps
             for c in range(steps):
-                w = D // steps
                 c0 = (i % J) * D + c * w
                 nc.scalar.copy(out=t_hx[:, c * w : (c + 1) * w], in_=x_tiles[i // J][:, c0 : c0 + w].bitcast(FP8))
 
-        def turn(i):
+        def turn_one(i):
             t_tr = ps_tr.tile([P, 512], F32, name="t_tr")
             tr[i] = t_tr
             words = hx[i][:].bitcast(F32)
@@ -122,13 +144,17 @@ def tile_mla_pa_t_w4_kernel(tc, h_bytes, h_scale, w_cq_words, w_cq_scales, w_q_w
                     c = (2 * u + g) * P
                     nc.tensor.transpose(t_tr[:, c : c + P], words[:, 256 * g + u : 256 * (g + 1) : 2], ident[:])
 
+        def turn(i):
+            if i % 2 == 0:
+                turn_one(i)
+                turn_one(i + 1)
+
         def empty(i):
             t_hq = work.tile([P, 2, P, 4], BF16, name="t_hq", align_bytes=64)
             hq[i] = t_hq
-            src = tr[i][:].bitcast(BF16).rearrange("p (u g r e) -> p g r u e", u=2, g=2, e=2)
             nc.vector.tensor_tensor(
                 out=t_hq[:].rearrange("p g r (u e) -> p g r u e", u=2),
-                in0=src,
+                in0=tr[i][:].bitcast(BF16).rearrange("p (u g r e) -> p g r u e", u=2, g=2, e=2),
                 in1=sc[:].rearrange("p (g o u e) -> p g o u e", g=2, o=1, u=2).to_broadcast([P, 2, P, 2, 2]),
                 op=ALU.mult,
             )
@@ -187,16 +213,16 @@ def tile_mla_pa_t_w4_kernel(tc, h_bytes, h_scale, w_cq_words, w_cq_scales, w_q_w
                 )
 
             product(t_u[:], wrw[:], wrs[:], True, True)
+            product(t_a[:], wqw[:, 0, :], ws[:, 2, :], True, True)
             for c in range(2):
                 for e in range(2):
                     n0 = 256 * e + P * c
                     product(t_s[:, P * c : P * (c + 1)], wrw[:, 2 * n0 : 2 * n0 + 256], wrs[:, n0 : n0 + P], e == 0, e == 1)
-            product(t_a[:], wqw[:, 0, :], ws[:, 2, :], True, True)
 
         def copy_a(i):
             if i >= TILES - 2:
-                t_last = outs.tile([P, NH, 1, 256], F32, name="t_last")
-                osb[i] = t_last[:, :, 0, :]
+                t_one = outs.tile([P, NH, 1, 256], F32, name="t_one")
+                osb[i] = t_one[:, :, 0, :]
             elif i % 2 == 0:
                 t_out = outs.tile([P, NH, 2, 256], F32, name="t_out")
                 osb[i], osb[i + 1] = t_out[:, :, 0, :], t_out[:, :, 1, :]
@@ -204,34 +230,37 @@ def tile_mla_pa_t_w4_kernel(tc, h_bytes, h_scale, w_cq_words, w_cq_scales, w_q_w
             nc.scalar.copy(out=osb[i][:, :, 0:P], in_=aps[i][:].rearrange("p (n f) -> p n f", n=NH))
 
         def rope_mul(i):
-            a = (i // J % 2) * J + i % J
-            t_m1 = work.tile([P, 2, 256], F32, name="t_m1")
-            m1[i] = t_m1
+            t_m = work.tile([P, 512], F32, name="t_m")
+            mt[i] = t_m
             nc.vector.tensor_tensor(
-                out=m1[i][:].rearrange("p e (n i) -> p e n i", n=NH),
-                in0=ups[i][:].rearrange("p (e n i) -> p e n i", e=2, n=NH),
-                in1=pairs[:, :, a, :].rearrange("p e (o i) -> p e o i", o=1).to_broadcast([P, 2, NH, 64]),
+                out=t_m[:].rearrange("p (n i e) -> p n i e", n=NH, e=2),
+                in0=ups[i][:].rearrange("p (e n i) -> p n i e", e=2, n=NH),
+                in1=pairs[:, i % 8 : i % 8 + 1, :, :].to_broadcast([P, NH, 64, 2]),
                 op=ALU.mult,
             )
 
         def rope_sum(i):
-            a = (i // J % 2) * J + i % J
-            t_m2 = work.tile([P, 256], F32, name="t_m2")
-            m2[i] = t_m2
+            t_k = work.tile([P, 256], F32, name="t_k")
+            kt[i] = t_k
             nc.vector.tensor_tensor(
-                out=m2[i][:].rearrange("p (n i) -> p n i", n=NH),
+                out=t_k[:].rearrange("p (n i) -> p n i", n=NH),
                 in0=sps[i][:].rearrange("p (n i) -> p n i", n=NH),
-                in1=trig[:, 0, a, :].rearrange("p (o i) -> p o i", o=1).to_broadcast([P, NH, 64]),
+                in1=trig[:, 0, i % 8 : i % 8 + 1, :].to_broadcast([P, NH, 64]),
                 op=ALU.mult,
             )
 
-        def rope_add(i, eng):
+        def rope_add(i):
+            eng = nc.vector if i >= TILES - 1 else nc.gpsimd
             eng.tensor_tensor(
                 out=osb[i][:, :, P : 2 * P].rearrange("p n (i e) -> p n i e", e=2),
-                in0=m1[i][:].rearrange("p e (n i) -> p n i e", n=NH),
-                in1=m2[i][:].rearrange("p (n i o) -> p n i o", n=NH, o=1).to_broadcast([P, NH, 64, 2]),
+                in0=mt[i][:].rearrange("p (n i e) -> p n i e", n=NH, e=2),
+                in1=kt[i][:].rearrange("p (n i o) -> p n i o", n=NH, o=1).to_broadcast([P, NH, 64, 2]),
                 op=ALU.add,
             )
+
+        def rope_k(i):
+            rope_sum(i)
+            rope_add(i)
 
         def store(i):
             k, j = i // J, i % J
@@ -241,43 +270,27 @@ def tile_mla_pa_t_w4_kernel(tc, h_bytes, h_scale, w_cq_words, w_cq_scales, w_q_w
             elif i % 2 == 1:
                 nc.sync.dma_start(out=dst[:, :, (j - 1) * 256 : (j + 1) * 256], in_=opair[i][:].rearrange("p n j c -> p n (j c)"))
 
-        def table_vector():
-            flat = turns[:].rearrange("p a i -> p (a i)")
-            nc.vector.tensor_tensor(out=frac[:], in0=flat, in1=whole[:], op=ALU.subtract)
-            nc.vector.scalar_tensor_tensor(out=nfrac[:], in0=frac[:], scalar=0.5, in1=frac[:], op0=ALU.is_gt, op1=ALU.subtract)
-
-        def table_scalar():
-            flat = trig[:].rearrange("p k a i -> p k (a i)")
-            nc.scalar.activation(out=flat[:, 1, :], in_=nfrac[:], func=ACT.Sin, scale=TWO_PI)
-            nc.scalar.activation(out=flat[:, 2, :], in_=nfrac[:], func=ACT.Sin, scale=-TWO_PI)
-            nc.scalar.activation(out=afrac[:], in_=nfrac[:], func=ACT.Abs)
-            nc.scalar.activation(out=flat[:, 0, :], in_=afrac[:], func=ACT.Sin, scale=-TWO_PI, bias=TWO_PI / 4)
-            nc.gpsimd.tensor_tensor(out=pairs[:].rearrange("p k a i -> p k (a i)"), in0=flat[:, 1:3, :], in1=flat[:, 0:1, :].to_broadcast([P, 2, 512]), op=ALU.subtract)
-
-        def at(fn, i):
-            if 0 <= i < TILES:
-                fn(i)
-
+        stages = (
+            (rope_mul, 6),
+            (copy_cq, 5),
+            (turn, 2),
+            (quant_h, 3),
+            (mm1, 4),
+            (copy_a, 6),
+            (rope_k, 6),
+            (quant_c, 5),
+            (mm2, 5),
+            (empty, 2),
+            (widen, 0),
+        )
+        once = {order_cq_scales: 2, table_vector: 2, order_rope_weights: 3, table_scalar: 4}
         for s in range(TILES + 6):
-            at(empty, s - 2)
-            if s == 2:
-                nc.vector.tensor_copy(out=wcs[:].rearrange("p g (t m) -> p g t m", t=4), in_=ws[:, 0:2, :].rearrange("p g (m t) -> p g t m", t=4))
-            if s == 3:
-                order_rope_weights()
-                table_vector()
-            if s == 4:
-                table_scalar()
-            at(copy_cq, s - 4)
-            at(copy_a, s - 5)
-            at(rope_mul, s - 5)
-            at(quant_h, s - 3)
-            at(quant_c, s - 4)
-            at(rope_sum, s - 5)
-            if 0 <= s - 5 < TILES:
-                i = s - 5
-                rope_add(i, nc.vector if i >= TILES - 2 else nc.gpsimd)
-            at(widen, s)
-            at(turn, s - 1)
-            at(mm1, s - 3)
-            at(mm2, s - 4)
-            at(store, s - 5)
+            for fn, lag in stages:
+                if 0 <= s - lag < TILES:
+                    fn(s - lag)
+                if fn is empty:
+                    for extra, when in once.items():
+                        if when == s:
+                            extra()
+                if fn is rope_k and 0 <= s - lag < TILES:
+                    store(s - lag)

from contextlib import ExitStack

import concourse.mybir as mybir
from concourse.masks import make_identity

B, S, D, NH, DH, CQ, HR = 4, 1024, 1024, 4, 128, 512, 128
FLOPS = 2 * B * S * (D * CQ + CQ * NH * DH + CQ * NH * HR)

F32 = mybir.dt.float32
BF16 = mybir.dt.bfloat16
U32 = mybir.dt.uint32
I32 = mybir.dt.int32
U8 = mybir.dt.uint8
FP8 = mybir.dt.float8_e4m3fn
FP8X4 = mybir.dt.float8_e4m3fn_x4
FP4X4 = mybir.dt.float4_e2m1fn_x4
ALU = mybir.AluOpType
ACT = mybir.ActivationFunctionType

P = 128
J = 4
GROUPS = B * S // (P * J)
TILES = GROUPS * J
TWO_PI = 6.283185307179586
RATIO = 10000.0 ** (-1.0 / 64.0)


def tile_mla_pa_t_w4_kernel(tc, h_bytes, h_scale, w_cq_words, w_cq_scales, w_q_words, w_q_scales, w_qr_words, w_qr_scales, out):
    nc = tc.nc
    with ExitStack() as ctx:
        keep = ctx.enter_context(tc.tile_pool(name="keep", bufs=1))
        xpool = ctx.enter_context(tc.tile_pool(name="xpool", bufs=GROUPS))
        work = ctx.enter_context(tc.tile_pool(name="work", bufs=5))
        outs = ctx.enter_context(tc.tile_pool(name="outs", bufs=5))
        ps_tr = ctx.enter_context(tc.psum_pool(name="ps_tr", bufs=3))
        ps_cq = ctx.enter_context(tc.psum_pool(name="ps_cq", bufs=1))
        ps_u = ctx.enter_context(tc.psum_pool(name="ps_u", bufs=1))
        ps_s = ctx.enter_context(tc.psum_pool(name="ps_s", bufs=2))
        ps_a = ctx.enter_context(tc.psum_pool(name="ps_a", bufs=1))

        ident = keep.tile([P, P], F32, name="ident")
        make_identity(nc, ident[:])

        ctx.enter_context(tc.manual_schedule())

        ws = keep.tile([P, 4, CQ], U8, name="ws", align_bytes=256)
        nc.vector.memset(ws[:].rearrange("p a n -> p (a n)").bitcast(I32), 0)
        sc = keep.tile([P, 8], F32, name="sc")
        wraw = keep.tile([P, 2, 2 * CQ], U8, name="wraw", align_bytes=256)
        wcw = keep.tile([P, 2, 2 * CQ], U8, name="wcw", align_bytes=256)
        wcs = keep.tile([P, 2, CQ], U8, name="wcs", align_bytes=256)
        wqw = keep.tile([P, 2, 2 * CQ], U8, name="wqw", align_bytes=256)
        wrw = keep.tile([P, 2 * CQ], U8, name="wrw", align_bytes=256)
        wrs = keep.tile([P, CQ], U8, name="wrs", align_bytes=256)

        x_tiles = []
        for k in range(GROUPS):
            x_bytes = xpool.tile([P, J * D], U8, name="x_bytes", align_bytes=64)
            x_tiles.append(x_bytes)
        xs = [h_bytes[k // 2].rearrange("(f p j) d -> f p (j d)", p=P, j=J)[k % 2] for k in range(GROUPS)]
        nc.sync.dma_start(out=wraw[:, 0, :].bitcast(I32), in_=w_cq_words[0].bitcast(I32))
        nc.sync.dma_start(out=x_tiles[0][:, 0:D], in_=xs[0][:, 0:D])
        nc.sync.dma_start(out=wraw[:, 1, :].bitcast(I32), in_=w_cq_words[1].bitcast(I32))
        nc.sync.dma_start(out=sc[:].rearrange("p (g t) -> p g t", t=4), in_=h_scale.rearrange("a b (g p t) -> p (a b g) t", p=P, t=4))
        nc.sync.dma_start(out=x_tiles[0][:, D : 2 * D], in_=xs[0][:, D : 2 * D])
        for q in range(4):
            nc.sync.dma_start(out=ws[32 * q : 32 * q + 4, 0:2, :].bitcast(I32), in_=w_cq_scales[:, 4 * q : 4 * q + 4, :].rearrange("g q n -> q g n").bitcast(I32))
        nc.sync.dma_start(out=x_tiles[0][:, 2 * D : 4 * D], in_=xs[0][:, 2 * D : 4 * D])
        for q in range(4):
            nc.sync.dma_start(out=ws[32 * q : 32 * q + 4, 2, :].bitcast(I32), in_=w_q_scales[0, 4 * q : 4 * q + 4, :].bitcast(I32))
            nc.sync.dma_start(out=ws[32 * q : 32 * q + 4, 3, :].bitcast(I32), in_=w_qr_scales[0, 4 * q : 4 * q + 4, :].bitcast(I32))
        nc.sync.dma_start(out=wqw[:, 0, :].bitcast(I32), in_=w_q_words[0].bitcast(I32))
        nc.sync.dma_start(out=wqw[:, 1, :].bitcast(I32), in_=w_qr_words[0].bitcast(I32))
        for k in range(1, GROUPS):
            nc.sync.dma_start(out=x_tiles[k][:], in_=xs[k])

        zero = keep.tile([P, 1], F32, name="zero")
        dummy = keep.tile([P, 1], F32, name="dummy")
        nc.gpsimd.memset(zero[:], 0.0)
        nc.scalar.activation(out=dummy[:], in_=zero[:], func=ACT.Sin)
        pos = keep.tile([P, 8], F32, name="pos")
        nc.gpsimd.iota(pos[:], pattern=[[512, 2], [1, 4]], base=0, channel_multiplier=4, allow_small_or_imprecise_dtypes=True)
        turns = keep.tile([P, 8, 64], F32, name="turns")
        nc.gpsimd.tensor_scalar(turns[:, :, 0:1], pos[:].rearrange("p (a o) -> p a o", o=1), 1.0 / TWO_PI, 0.0, ALU.mult, ALU.add)
        w = 1
        while w < 64:
            nc.gpsimd.tensor_scalar(turns[:, :, w : 2 * w], turns[:, :, 0:w], RATIO**w, 0.0, ALU.mult, ALU.add)
            w *= 2
        whole = keep.tile([P, 512], I32, name="whole")
        nc.gpsimd.tensor_scalar(whole[:], turns[:].rearrange("p a i -> p (a i)"), 1.0, 0.0, ALU.mult, ALU.add)
        frac = keep.tile([P, 512], F32, name="frac")
        nfrac = keep.tile([P, 512], F32, name="nfrac")
        afrac = keep.tile([P, 512], F32, name="afrac")
        trig = keep.tile([P, 3, 8, 64], F32, name="trig")
        pairs = keep.tile([P, 8, 64, 2], F32, name="pairs")

        for g in range(2):
            nc.vector.tensor_copy(out=wcw[:, g, :].rearrange("p (t m b) -> p t m b", t=4, b=2), in_=wraw[:, g, :].rearrange("p (m t b) -> p t m b", t=4, b=2))

        def order_cq_scales():
            nc.vector.tensor_copy(out=wcs[:].rearrange("p g (t m) -> p g t m", t=4), in_=ws[:, 0:2, :].rearrange("p g (m t) -> p g t m", t=4))

        def order_rope_weights():
            for e in range(2):
                nc.vector.tensor_copy(out=wrw[:, CQ * (1 - e) : CQ * (2 - e)].rearrange("p (q b) -> p q b", b=2), in_=wqw[:, 1, :].rearrange("p (q e b) -> p e q b", e=2, b=2)[:, e])
            for e in range(2):
                nc.vector.tensor_copy(out=wrs[:, 256 * (1 - e) : 256 * (2 - e)], in_=ws[:, 3, :].rearrange("p (q e) -> p e q", e=2)[:, e])

        def table_vector():
            flat = turns[:].rearrange("p a i -> p (a i)")
            nc.vector.tensor_tensor(out=frac[:], in0=flat, in1=whole[:], op=ALU.subtract)
            nc.vector.scalar_tensor_tensor(out=nfrac[:], in0=frac[:], scalar=0.5, in1=frac[:], op0=ALU.is_gt, op1=ALU.subtract)

        def table_scalar():
            flat = trig[:].rearrange("p k a i -> p k (a i)")
            nc.scalar.activation(out=flat[:, 1, :], in_=nfrac[:], func=ACT.Sin, scale=TWO_PI)
            nc.scalar.activation(out=flat[:, 2, :], in_=nfrac[:], func=ACT.Sin, scale=-TWO_PI)
            nc.scalar.activation(out=afrac[:], in_=nfrac[:], func=ACT.Abs)
            nc.scalar.activation(out=flat[:, 0, :], in_=afrac[:], func=ACT.Sin, scale=-TWO_PI, bias=TWO_PI / 4)
            nc.vector.tensor_tensor(
                out=pairs[:].rearrange("p a i k -> p (a i) k"),
                in0=flat[:, 1:3, :].rearrange("p k q -> p q k"),
                in1=flat[:, 0, :].rearrange("p (q o) -> p q o", o=1).to_broadcast([P, 512, 2]),
                op=ALU.subtract,
            )

        hx, tr, hq, hc, hs, cq, cqb, cc, cs, aps, ups, sps, mt, kt, osb, opair = ({} for n in range(16))

        def widen(i):
            t_hx = work.tile([P, D], BF16, name="t_hx")
            hx[i] = t_hx
            steps = 2 if i == 0 else 1
            w = D // steps
            for c in range(steps):
                c0 = (i % J) * D + c * w
                nc.scalar.copy(out=t_hx[:, c * w : (c + 1) * w], in_=x_tiles[i // J][:, c0 : c0 + w].bitcast(FP8))

        def turn_one(i):
            t_tr = ps_tr.tile([P, 512], F32, name="t_tr")
            tr[i] = t_tr
            words = hx[i][:].bitcast(F32)
            for g in range(2):
                for u in range(2):
                    c = (2 * u + g) * P
                    nc.tensor.transpose(t_tr[:, c : c + P], words[:, 256 * g + u : 256 * (g + 1) : 2], ident[:])

        def turn(i):
            if i % 2 == 0:
                turn_one(i)
                turn_one(i + 1)

        def empty(i):
            t_hq = work.tile([P, 2, P, 4], BF16, name="t_hq", align_bytes=64)
            hq[i] = t_hq
            nc.vector.tensor_tensor(
                out=t_hq[:].rearrange("p g r (u e) -> p g r u e", u=2),
                in0=tr[i][:].bitcast(BF16).rearrange("p (u g r e) -> p g r u e", u=2, g=2, e=2),
                in1=sc[:].rearrange("p (g o u e) -> p g o u e", g=2, o=1, u=2).to_broadcast([P, 2, P, 2, 2]),
                op=ALU.mult,
            )

        def quant_h(i):
            t_hc = work.tile([P, 2, P], U32, name="t_hc", align_bytes=64)
            t_hs = work.tile([P, 2, P], U8, name="t_hs", align_bytes=64)
            hc[i], hs[i] = t_hc, t_hs
            nc.vector.quantize_mx(
                out=t_hc[:].rearrange("p g r -> p (g r)").bitcast(FP8X4),
                scales=t_hs[:].rearrange("p g r -> p (g r)"),
                in_=hq[i][:].rearrange("p g r t -> p (g r t)"),
            )

        def mm1(i):
            t_cq = ps_cq.tile([P, 4, P], F32, name="t_cq")
            cq[i] = t_cq
            for t in range(4):
                for g in range(2):
                    nc.tensor.matmul_mx(
                        out=t_cq[:, t, :],
                        lhsT=wcw[:, g, 256 * t : 256 * (t + 1)].bitcast(FP4X4),
                        lhsT_scale=wcs[:, g, P * t : P * (t + 1)],
                        rhs=hc[i][:, g, :].bitcast(FP8X4),
                        rhs_scale=hs[i][:, g, :],
                        start=(g == 0),
                        stop=(g == 1),
                    )

        def copy_cq(i):
            t_cqb = work.tile([P, P, 4], BF16, name="t_cqb", align_bytes=64)
            cqb[i] = t_cqb
            nc.scalar.copy(out=t_cqb[:], in_=cq[i][:].rearrange("p t n -> p n t"))

        def quant_c(i):
            t_cc = work.tile([P, P], U32, name="t_cc", align_bytes=64)
            t_cs = work.tile([P, P], U8, name="t_cs", align_bytes=64)
            cc[i], cs[i] = t_cc, t_cs
            nc.vector.quantize_mx(out=t_cc[:].bitcast(FP8X4), scales=t_cs[:], in_=cqb[i][:].rearrange("p n t -> p (n t)"))

        def mm2(i):
            t_u = ps_u.tile([P, 512], F32, name="t_u")
            t_s = ps_s.tile([P, 256], F32, name="t_s")
            t_a = ps_a.tile([P, 512], F32, name="t_a")
            ups[i], sps[i], aps[i] = t_u, t_s, t_a

            def product(dst, words, scales, start, stop):
                nc.tensor.matmul_mx(
                    out=dst,
                    lhsT=cc[i][:].bitcast(FP8X4),
                    lhsT_scale=cs[i][:],
                    rhs=words.bitcast(FP4X4),
                    rhs_scale=scales,
                    start=start,
                    stop=stop,
                )

            product(t_u[:], wrw[:], wrs[:], True, True)
            product(t_a[:], wqw[:, 0, :], ws[:, 2, :], True, True)
            for c in range(2):
                for e in range(2):
                    n0 = 256 * e + P * c
                    product(t_s[:, P * c : P * (c + 1)], wrw[:, 2 * n0 : 2 * n0 + 256], wrs[:, n0 : n0 + P], e == 0, e == 1)

        def copy_a(i):
            if i >= TILES - 2:
                t_one = outs.tile([P, NH, 1, 256], F32, name="t_one")
                osb[i] = t_one[:, :, 0, :]
            elif i % 2 == 0:
                t_out = outs.tile([P, NH, 2, 256], F32, name="t_out")
                osb[i], osb[i + 1] = t_out[:, :, 0, :], t_out[:, :, 1, :]
                opair[i + 1] = t_out
            nc.scalar.copy(out=osb[i][:, :, 0:P], in_=aps[i][:].rearrange("p (n f) -> p n f", n=NH))

        def rope_mul(i):
            t_m = work.tile([P, 512], F32, name="t_m")
            mt[i] = t_m
            nc.vector.tensor_tensor(
                out=t_m[:].rearrange("p (n i e) -> p n i e", n=NH, e=2),
                in0=ups[i][:].rearrange("p (e n i) -> p n i e", e=2, n=NH),
                in1=pairs[:, i % 8 : i % 8 + 1, :, :].to_broadcast([P, NH, 64, 2]),
                op=ALU.mult,
            )

        def rope_sum(i):
            t_k = work.tile([P, 256], F32, name="t_k")
            kt[i] = t_k
            nc.vector.tensor_tensor(
                out=t_k[:].rearrange("p (n i) -> p n i", n=NH),
                in0=sps[i][:].rearrange("p (n i) -> p n i", n=NH),
                in1=trig[:, 0, i % 8 : i % 8 + 1, :].to_broadcast([P, NH, 64]),
                op=ALU.mult,
            )

        def rope_add(i):
            eng = nc.vector if i >= TILES - 1 else nc.gpsimd
            eng.tensor_tensor(
                out=osb[i][:, :, P : 2 * P].rearrange("p n (i e) -> p n i e", e=2),
                in0=mt[i][:].rearrange("p (n i e) -> p n i e", n=NH, e=2),
                in1=kt[i][:].rearrange("p (n i o) -> p n i o", n=NH, o=1).to_broadcast([P, NH, 64, 2]),
                op=ALU.add,
            )

        def rope_k(i):
            rope_sum(i)
            rope_add(i)

        def store(i):
            k, j = i // J, i % J
            dst = out[k // 2].rearrange("n (f p j) c -> f p n (j c)", p=P, j=J)[k % 2]
            if i >= TILES - 2:
                nc.sync.dma_start(out=dst[:, :, j * 256 : (j + 1) * 256], in_=osb[i])
            elif i % 2 == 1:
                nc.sync.dma_start(out=dst[:, :, (j - 1) * 256 : (j + 1) * 256], in_=opair[i][:].rearrange("p n j c -> p n (j c)"))

        stages = (
            (rope_mul, 6),
            (copy_cq, 5),
            (turn, 2),
            (quant_h, 3),
            (mm1, 4),
            (copy_a, 6),
            (rope_k, 6),
            (quant_c, 5),
            (mm2, 5),
            (empty, 2),
            (widen, 0),
        )
        once = {order_cq_scales: 2, table_vector: 2, order_rope_weights: 3, table_scalar: 4}
        for s in range(TILES + 6):
            for fn, lag in stages:
                if 0 <= s - lag < TILES:
                    fn(s - lag)
                if fn is empty:
                    for extra, when in once.items():
                        if when == s:
                            extra()
                if fn is rope_k and 0 <= s - lag < TILES:
                    store(s - lag)
